import numpy as np
import ml_dtypes


def mxq(x, axis, fmt="e4m3"):
    dtype, down = {"e4m3": (ml_dtypes.float8_e4m3fn, 7), "e5m2": (ml_dtypes.float8_e5m2, 14)}[fmt]
    v = np.moveaxis(np.asarray(x, np.float32).astype(ml_dtypes.bfloat16).astype(np.float64), axis, -1)
    blocks = v.reshape(v.shape[:-1] + (-1, 32))
    amax = np.abs(blocks).max(-1, keepdims=True)
    byte = np.maximum(np.where(amax > 0, np.frexp(amax)[1] - 1 + 127, 0) - down, 1)
    scale = np.exp2(byte - 127.0)
    codes = (blocks / scale).astype(np.float32).astype(dtype).astype(np.float64)
    return np.moveaxis((codes * scale).reshape(v.shape), -1, axis)


WIDE = False


def mx_kscale(k):
    if not WIDE:
        return np.ones(k)
    levels = np.array([10, -10, 5, -5, 0])
    if k % 512:
        return np.exp2(np.random.permutation(np.resize(levels, k // 32))).repeat(32)
    a = np.empty((k // 512, 16))
    for p in range(k // 512):
        a[p, :8] = np.random.permutation(np.resize(levels, 8))
        for g in range(8):
            far = levels[np.abs(levels - a[p, g]) >= 10]
            a[p, g + 8] = far[np.random.randint(len(far))]
    return np.exp2(a.ravel()).repeat(32)


BF16 = ml_dtypes.bfloat16


def bf(x):
    return np.asarray(x, np.float32).astype(BF16)


def f64(x):
    return np.asarray(x).astype(np.float64)


B, H, L, E, QD = 16, 1, 128, 2048, 128
EPS = 1e-5


def build_decay_mask(num_heads, max_len):
    r = f64(np.arange(max_len))
    dec = np.array([1.0 - 2.0 ** (-5 - h) for h in range(num_heads)])
    expo = r[None, :] - r[:, None]
    return np.where(r[:, None] >= r[None, :], dec[:, None, None] ** expo[None], 0.0)


def setup_inputs():
    s = mx_kscale(E)
    kv = (0.1 + 0.32 * np.random.standard_normal((B, H, L, QD))) * (0.1 + 0.32 * np.random.standard_normal((B, H, L, QD)))
    return {"x": bf(np.random.standard_normal((B, H, L, E)) * s),
            "Wq": bf(np.random.standard_normal((QD, E)) / np.sqrt(E) / s),
            "bq": bf(0.3 + 0.3 * np.random.standard_normal(QD)),
            "kv": bf(kv),
            "decay_mask": bf(build_decay_mask(H, L))}


def reference(x, Wq, bq, kv, decay_mask):
    b, h, l, e = x.shape
    Q = (mxq(f64(x), 3, "e4m3") @ mxq(f64(Wq), 1, "e4m3").T) + f64(bq)
    D = f64(decay_mask)[0, :l, :l]
    y = Q * (f64(kv) @ D.T)
    mean = y.mean(axis=(2, 3), keepdims=True)
    var = ((y - mean) ** 2).mean(axis=(2, 3), keepdims=True)
    y = (y - mean) / np.sqrt(var + EPS)
    return y.reshape(b, l, -1)

@@ -1,0 +1,277 @@
+from contextlib import ExitStack
+
+import concourse.mybir as mybir
+from concourse.masks import make_identity
+
+F32 = mybir.dt.float32
+BF16 = mybir.dt.bfloat16
+U32 = mybir.dt.uint32
+U8 = mybir.dt.uint8
+FP8X4 = mybir.dt.float8_e4m3fn_x4
+ALU = mybir.AluOpType
+ACT = mybir.ActivationFunctionType
+
+P = 128
+TOKENS = 16 * 128
+E = 2048
+PACK = 4
+PASSES = E // (P * PACK)
+WORDS = P
+BANK_PLANES = 4
+HALVES = E // 2 // (WORDS * BANK_PLANES)
+SLOTS = 4
+GROUPS = TOKENS // (P * SLOTS)
+CHUNK_SLOTS = 2
+CHUNKS = SLOTS // CHUNK_SLOTS
+SAMPLE_PARTITIONS = P // SLOTS
+SAMPLE_SIZE = 128 * 128
+EPS = 1e-5
+VECTOR_SHARE = 8
+
+FLOPS = 2 * TOKENS * E * P + 2 * TOKENS * P * P
+
+
+def tile_parallelretention_pb_kernel(tc, x, Wq, bq, kv, decay_mask, out):
+    nc = tc.nc
+    x_slots = x.flatten_outer_dims().rearrange("(g p s) k -> g p s k", p=P, s=SLOTS)
+    kv_slots = kv.flatten_outer_dims().rearrange("(g p s) k -> p g s k", p=P, s=SLOTS)
+    out_slots = out.flatten_outer_dims().rearrange("(g p s) q -> g p s q", p=P, s=SLOTS)
+
+    with ExitStack() as ctx:
+        const = ctx.enter_context(tc.tile_pool(name="const", bufs=1))
+        x_pool = ctx.enter_context(tc.tile_pool(name="x_pool", bufs=GROUPS * SLOTS))
+        grouped_pool = ctx.enter_context(tc.tile_pool(name="grouped_pool", bufs=3))
+        mx_pool = ctx.enter_context(tc.tile_pool(name="mx_pool", bufs=6))
+        work = ctx.enter_context(tc.tile_pool(name="work", bufs=3))
+        small = ctx.enter_context(tc.tile_pool(name="small", bufs=3))
+        ring = ctx.enter_context(tc.psum_pool(name="ring", bufs=5))
+        qg_psum = ctx.enter_context(tc.psum_pool(name="qg_psum", bufs=2))
+        sum_psum = ctx.enter_context(tc.psum_pool(name="sum_psum", bufs=1))
+
+        wq_rows = const.tile([P, E], BF16)
+        decay_rows = const.tile([P, P], BF16)
+        bias_rows = const.tile([P, P], BF16)
+        kv_rows = const.tile([P, GROUPS, SLOTS, P], BF16)
+        x_rows = {}
+
+        def load_token_tile(g, s):
+            rows = x_pool.tile([P, E], BF16, name="x_tile")
+            nc.sync.dma_start(out=rows[:], in_=x_slots[g][:, s, :])
+            x_rows[(g, s)] = rows
+
+        nc.vector.memset(bias_rows[:], 0.0)
+        nc.sync.dma_start(out=wq_rows[:], in_=Wq)
+        load_token_tile(0, 0)
+        load_token_tile(0, 1)
+        nc.sync.dma_start(out=decay_rows[:], in_=decay_mask.flatten_outer_dims())
+        nc.sync.dma_start(out=bias_rows[0:1, :], in_=bq.unsqueeze(0))
+        nc.sync.dma_start(out=kv_rows[:], in_=kv_slots)
+        for g in range(GROUPS):
+            for s in range(SLOTS):
+                if (g, s) not in x_rows:
+                    load_token_tile(g, s)
+
+        ident_f32 = const.tile([P, P], F32)
+        make_identity(nc, ident_f32[:])
+        ident_bf16 = const.tile([P, P], BF16)
+        make_identity(nc, ident_bf16[:])
+        ones_bf16 = const.tile([P, P], BF16)
+        nc.vector.memset(ones_bf16[:], 1.0)
+        eps_column = const.tile([P, 1], F32)
+        nc.vector.memset(eps_column[:], EPS)
+        sample_mean = const.tile([P, P], F32)
+        nc.vector.memset(sample_mean[:], 0.0)
+        for n in range(SLOTS):
+            rows = slice(n * SAMPLE_PARTITIONS, (n + 1) * SAMPLE_PARTITIONS)
+            nc.vector.memset(sample_mean[rows, rows], 1.0 / SAMPLE_SIZE)
+        table_warmer = const.tile([P, 1], F32)
+        nc.scalar.activation(out=table_warmer[:], in_=eps_column[:], func=ACT.Abs_reciprocal_sqrt)
+
+        banks_emptied = []
+
+        def transpose_words(words):
+            banks = []
+            for half in range(HALVES):
+                bank = ring.tile([P, BANK_PLANES, P], F32, name="word_bank", tag="ring")
+                for plane in range(BANK_PLANES):
+                    k_pass, u = divmod(half * BANK_PLANES + plane, 2)
+                    pair_words = slice(k_pass * 2 * WORDS + u, (k_pass + 1) * 2 * WORDS, 2)
+                    nc.tensor.transpose(bank[:, plane, :], words[:, pair_words], ident_f32[:])
+                banks.append(bank)
+            return banks
+
+        def regroup(banks):
+            grouped = grouped_pool.tile([P, PASSES, P, PACK], BF16, name="grouped", align_bytes=64)
+            passes_per_bank = PASSES // HALVES
+            for half in range(HALVES):
+                first = half * passes_per_bank
+                side_by_side = grouped[:].bitcast(F32)[:, first : first + passes_per_bank, :, :]
+                planes = banks[half][:].rearrange("p (g u) r -> p g r u", u=PACK // 2)
+                banks_emptied.append(half)
+                if len(banks_emptied) % VECTOR_SHARE == 0:
+                    nc.vector.tensor_copy(out=side_by_side, in_=planes)
+                else:
+                    nc.scalar.copy(out=side_by_side, in_=planes)
+            return grouped
+
+        def quantise(grouped, codes, scales):
+            nc.vector.quantize_mx(
+                out=codes[:].bitcast(FP8X4),
+                scales=scales[:],
+                in_=grouped[:].rearrange("p g r t -> p (g r t)"),
+            )
+
+        wq_codes = const.tile([P, PASSES * P], U32, align_bytes=64)
+        wq_scales = const.tile([P, PASSES * P], U8, align_bytes=64)
+        quantise(regroup(transpose_words(wq_rows[:].bitcast(F32))), wq_codes, wq_scales)
+
+        word_banks = {}
+        x_mx = {}
+        q_bank = {}
+        g_bank = {}
+        y_tile = {}
+        row_sums = {}
+        sums_bank = {}
+        mean_column = {}
+        square_sums = {}
+        kv_t = const.tile([P, GROUPS, SLOTS, P], BF16)
+        decay_t = const.tile([P, P], BF16)
+        bias_all = const.tile([P, P], F32)
+
+        def live(g):
+            return 0 <= g < GROUPS
+
+        def prepare_kv():
+            groups_per_bank = 2
+            for first in range(0, GROUPS, groups_per_bank):
+                kv_bank = ring.tile([P, groups_per_bank, SLOTS, P], BF16, name="kv_bank", tag="ring")
+                for g in range(groups_per_bank):
+                    for s in range(SLOTS):
+                        nc.tensor.transpose(kv_bank[:, g, s, :], kv_rows[:, first + g, s, :], ident_bf16[:])
+                nc.vector.tensor_copy(out=kv_t[:, first : first + groups_per_bank, :, :], in_=kv_bank[:])
+            decay_bank = ring.tile([P, P], BF16, name="decay_bank", tag="ring")
+            nc.tensor.transpose(decay_bank[:], decay_rows[:], ident_bf16[:])
+            nc.vector.tensor_copy(out=decay_t[:], in_=decay_bank[:])
+            bias_bank = ring.tile([P, P], F32, name="bias_bank", tag="ring")
+            nc.tensor.matmul(out=bias_bank[:], lhsT=ones_bf16[:], rhs=bias_rows[:], start=True, stop=True)
+            nc.vector.tensor_copy(out=bias_all[:], in_=bias_bank[:])
+
+        def transposes(g, c):
+            if live(g):
+                for j in range(CHUNK_SLOTS):
+                    word_banks[(g, c, j)] = transpose_words(x_rows[(g, c * CHUNK_SLOTS + j)][:].bitcast(F32))
+
+        def pack(g, c, j):
+            if live(g):
+                codes = mx_pool.tile([P, PASSES * P], U32, name="x_codes", align_bytes=64)
+                scales = mx_pool.tile([P, PASSES * P], U8, name="x_scales", align_bytes=64)
+                quantise(regroup(word_banks[(g, c, j)]), codes, scales)
+                x_mx[(g, c, j)] = (codes, scales)
+
+        def products(g, c):
+            if not live(g):
+                return
+            qg_bank = qg_psum.tile([P, 2, CHUNK_SLOTS, P], F32, name="qg_bank")
+            q_bank[(g, c)] = qg_bank[:, 0, :, :]
+            g_bank[(g, c)] = qg_bank[:, 1, :, :]
+            for j in range(CHUNK_SLOTS):
+                codes, scales = x_mx[(g, c, j)]
+                for k_pass in range(PASSES):
+                    cols = slice(k_pass * P, (k_pass + 1) * P)
+                    nc.tensor.matmul_mx(
+                        out=q_bank[(g, c)][:, j, :],
+                        lhsT=codes[:, cols].bitcast(FP8X4),
+                        lhsT_scale=scales[:, cols],
+                        rhs=wq_codes[:, cols].bitcast(FP8X4),
+                        rhs_scale=wq_scales[:, cols],
+                        start=(k_pass == 0),
+                        stop=(k_pass == PASSES - 1),
+                    )
+            for j in range(CHUNK_SLOTS):
+                nc.tensor.matmul(
+                    out=g_bank[(g, c)][:, j, :], lhsT=kv_t[:, g, c * CHUNK_SLOTS + j, :], rhs=decay_t[:], start=True, stop=True
+                )
+
+        def weigh(g, c):
+            if not live(g):
+                return
+            if c == 0:
+                y_tile[g] = work.tile([P, SLOTS, P], F32, name="y_tile")
+                row_sums[g] = small.tile([P, CHUNKS], F32, name="row_sums")
+            slots = slice(c * CHUNK_SLOTS, (c + 1) * CHUNK_SLOTS)
+            biased = work.tile([P, CHUNK_SLOTS, P], F32, name="biased")
+            nc.vector.tensor_tensor(
+                out=biased[:],
+                in0=q_bank[(g, c)],
+                in1=bias_all[:].unsqueeze(1).to_broadcast([P, CHUNK_SLOTS, P]),
+                op=ALU.add,
+            )
+            nc.vector.scalar_tensor_tensor(
+                out=y_tile[g][:, slots, :].rearrange("p s q -> p (s q)"),
+                in0=biased[:].rearrange("p s q -> p (s q)"),
+                scalar=1.0,
+                in1=g_bank[(g, c)].rearrange("p s q -> p (s q)"),
+                op0=ALU.mult,
+                op1=ALU.mult,
+                accum_out=row_sums[g][:, c : c + 1],
+            )
+
+        def mean_of(g):
+            if not live(g):
+                return
+            sums_bank[g] = sum_psum.tile([P, CHUNKS + 1], F32, name="sums_bank")
+            nc.tensor.matmul(out=sums_bank[g][:, 0:CHUNKS], lhsT=sample_mean[:], rhs=row_sums[g][:], start=True, stop=True)
+            mean_column[g] = small.tile([P, 1], F32, name="mean_column")
+            nc.vector.tensor_reduce(out=mean_column[g][:], in_=sums_bank[g][:, 0:CHUNKS], axis=mybir.AxisListType.X, op=ALU.add)
+
+        def squares(g):
+            if not live(g):
+                return
+            squared = work.tile([P, SLOTS * P], F32, name="squared")
+            square_sums[g] = small.tile([P, 1], F32, name="square_sums")
+            nc.scalar.activation(
+                out=squared[:],
+                in_=y_tile[g][:].rearrange("p s q -> p (s q)"),
+                func=ACT.Square,
+                bias=mean_column[g][:],
+                scale=-1.0,
+                accum_out=square_sums[g][:],
+            )
+
+        def variance_of(g):
+            if live(g):
+                nc.tensor.matmul(
+                    out=sums_bank[g][:, CHUNKS : CHUNKS + 1], lhsT=sample_mean[:], rhs=square_sums[g][:], start=True, stop=True
+                )
+
+        def finish(g):
+            if not live(g):
+                return
+            rstd = small.tile([P, 1], F32, name="rstd")
+            nc.scalar.activation(
+                out=rstd[:], in_=sums_bank[g][:, CHUNKS : CHUNKS + 1], func=ACT.Abs_reciprocal_sqrt, bias=eps_column[:]
+            )
+            res = work.tile([P, SLOTS, P], F32, name="res")
+            nc.vector.tensor_scalar(
+                out=res[:], in0=y_tile[g][:], scalar1=mean_column[g][:], scalar2=rstd[:], op0=ALU.subtract, op1=ALU.mult
+            )
+            nc.sync.dma_start(out=out_slots[g], in_=res[:])
+
+        for i in range(GROUPS + 2):
+            transposes(i, 0)
+            variance_of(i - 2)
+            products(i - 1, 1)
+            pack(i, 0, 0)
+            weigh(i - 1, 1)
+            pack(i, 0, 1)
+            finish(i - 2)
+            if i == 0:
+                prepare_kv()
+
+            transposes(i, 1)
+            mean_of(i - 1)
+            products(i, 0)
+            pack(i, 1, 0)
+            squares(i - 1)
+            weigh(i, 0)
+            pack(i, 1, 1)

@@ -19,13 +19,12 @@ PASSES = E // (P * PACK)
 WORDS = P
 BANK_PLANES = 4
 HALVES = E // 2 // (WORDS * BANK_PLANES)
-SLOTS = 4
-GROUPS = TOKENS // (P * SLOTS)
-CHUNK_SLOTS = 2
-CHUNKS = SLOTS // CHUNK_SLOTS
+SLOTS = 2
+CHUNKS = TOKENS // (P * SLOTS)
 SAMPLE_PARTITIONS = P // SLOTS
 SAMPLE_SIZE = 128 * 128
 EPS = 1e-5
+KV_AFTER = 2
 VECTOR_SHARE = 8
 
 FLOPS = 2 * TOKENS * E * P + 2 * TOKENS * P * P
@@ -33,17 +32,16 @@ FLOPS = 2 * TOKENS * E * P + 2 * TOKENS * P * P
 
 def tile_parallelretention_pb_kernel(tc, x, Wq, bq, kv, decay_mask, out):
     nc = tc.nc
-    x_slots = x.flatten_outer_dims().rearrange("(g p s) k -> g p s k", p=P, s=SLOTS)
-    kv_slots = kv.flatten_outer_dims().rearrange("(g p s) k -> p g s k", p=P, s=SLOTS)
-    out_slots = out.flatten_outer_dims().rearrange("(g p s) q -> g p s q", p=P, s=SLOTS)
+    x_slots = x.flatten_outer_dims().rearrange("(c p s) k -> c p s k", p=P, s=SLOTS)
+    kv_slots = kv.flatten_outer_dims().rearrange("(c p s) k -> p c s k", p=P, s=SLOTS)
+    out_slots = out.flatten_outer_dims().rearrange("(c p s) q -> c p s q", p=P, s=SLOTS)
 
     with ExitStack() as ctx:
         const = ctx.enter_context(tc.tile_pool(name="const", bufs=1))
-        x_pool = ctx.enter_context(tc.tile_pool(name="x_pool", bufs=GROUPS * SLOTS))
-        grouped_pool = ctx.enter_context(tc.tile_pool(name="grouped_pool", bufs=3))
-        mx_pool = ctx.enter_context(tc.tile_pool(name="mx_pool", bufs=6))
-        work = ctx.enter_context(tc.tile_pool(name="work", bufs=3))
-        small = ctx.enter_context(tc.tile_pool(name="small", bufs=3))
+        x_pool = ctx.enter_context(tc.tile_pool(name="x_pool", bufs=CHUNKS * SLOTS))
+        grouped_pool = ctx.enter_context(tc.tile_pool(name="grouped_pool", bufs=4))
+        mx_pool = ctx.enter_context(tc.tile_pool(name="mx_pool", bufs=8))
+        work = ctx.enter_context(tc.tile_pool(name="work", bufs=CHUNKS))
         ring = ctx.enter_context(tc.psum_pool(name="ring", bufs=5))
         qg_psum = ctx.enter_context(tc.psum_pool(name="qg_psum", bufs=2))
         sum_psum = ctx.enter_context(tc.psum_pool(name="sum_psum", bufs=1))
@@ -51,25 +49,25 @@ def tile_parallelretention_pb_kernel(tc, x, Wq, bq, kv, decay_mask, out):
         wq_rows = const.tile([P, E], BF16)
         decay_rows = const.tile([P, P], BF16)
         bias_rows = const.tile([P, P], BF16)
-        kv_rows = const.tile([P, GROUPS, SLOTS, P], BF16)
+        kv_rows = const.tile([P, CHUNKS, SLOTS, P], BF16)
         x_rows = {}
 
-        def load_token_tile(g, s):
+        def load_token_tile(c, s):
             rows = x_pool.tile([P, E], BF16, name="x_tile")
-            nc.sync.dma_start(out=rows[:], in_=x_slots[g][:, s, :])
-            x_rows[(g, s)] = rows
+            nc.sync.dma_start(out=rows[:], in_=x_slots[c][:, s, :])
+            x_rows[(c, s)] = rows
 
         nc.vector.memset(bias_rows[:], 0.0)
-        nc.sync.dma_start(out=wq_rows[:], in_=Wq)
-        load_token_tile(0, 0)
-        load_token_tile(0, 1)
-        nc.sync.dma_start(out=decay_rows[:], in_=decay_mask.flatten_outer_dims())
-        nc.sync.dma_start(out=bias_rows[0:1, :], in_=bq.unsqueeze(0))
-        nc.sync.dma_start(out=kv_rows[:], in_=kv_slots)
-        for g in range(GROUPS):
+        for half in range(HALVES):
+            columns = slice(half * E // HALVES, (half + 1) * E // HALVES)
+            nc.sync.dma_start(out=wq_rows[:, columns], in_=Wq[:, columns])
+        for c in range(CHUNKS):
             for s in range(SLOTS):
-                if (g, s) not in x_rows:
-                    load_token_tile(g, s)
+                load_token_tile(c, s)
+            if c == KV_AFTER:
+                nc.sync.dma_start(out=decay_rows[:], in_=decay_mask.flatten_outer_dims())
+                nc.sync.dma_start(out=bias_rows[0:1, :], in_=bq.unsqueeze(0))
+                nc.sync.dma_start(out=kv_rows[:], in_=kv_slots)
 
         ident_f32 = const.tile([P, P], F32)
         make_identity(nc, ident_f32[:])
@@ -108,7 +106,7 @@ def tile_parallelretention_pb_kernel(tc, x, Wq, bq, kv, decay_mask, out):
                 side_by_side = grouped[:].bitcast(F32)[:, first : first + passes_per_bank, :, :]
                 planes = banks[half][:].rearrange("p (g u) r -> p g r u", u=PACK // 2)
                 banks_emptied.append(half)
-                if len(banks_emptied) % VECTOR_SHARE == 0:
+                if len(banks_emptied) % VECTOR_SHARE == 2:
                     nc.vector.tensor_copy(out=side_by_side, in_=planes)
                 else:
                     nc.scalar.copy(out=side_by_side, in_=planes)
@@ -123,32 +121,34 @@ def tile_parallelretention_pb_kernel(tc, x, Wq, bq, kv, decay_mask, out):
 
         wq_codes = const.tile([P, PASSES * P], U32, align_bytes=64)
         wq_scales = const.tile([P, PASSES * P], U8, align_bytes=64)
-        quantise(regroup(transpose_words(wq_rows[:].bitcast(F32))), wq_codes, wq_scales)
 
         word_banks = {}
+        grouped_tile = {}
         x_mx = {}
         q_bank = {}
         g_bank = {}
+        biased_tile = {}
         y_tile = {}
-        row_sums = {}
-        sums_bank = {}
-        mean_column = {}
-        square_sums = {}
-        kv_t = const.tile([P, GROUPS, SLOTS, P], BF16)
+        kv_t = const.tile([P, CHUNKS, SLOTS, P], BF16)
+        row_sums = const.tile([P, CHUNKS], F32)
+        mean_columns = const.tile([P, CHUNKS], F32)
+        square_sums = const.tile([P, CHUNKS], F32)
+        rstd_columns = const.tile([P, CHUNKS], F32)
+        sums_bank = sum_psum.tile([P, 2, CHUNKS], F32, name="sums_bank")
         decay_t = const.tile([P, P], BF16)
         bias_all = const.tile([P, P], F32)
 
-        def live(g):
-            return 0 <= g < GROUPS
+        def live(c):
+            return 0 <= c < CHUNKS
 
-        def prepare_kv():
-            groups_per_bank = 2
-            for first in range(0, GROUPS, groups_per_bank):
-                kv_bank = ring.tile([P, groups_per_bank, SLOTS, P], BF16, name="kv_bank", tag="ring")
-                for g in range(groups_per_bank):
-                    for s in range(SLOTS):
-                        nc.tensor.transpose(kv_bank[:, g, s, :], kv_rows[:, first + g, s, :], ident_bf16[:])
-                nc.vector.tensor_copy(out=kv_t[:, first : first + groups_per_bank, :, :], in_=kv_bank[:])
+        def prepare_kv(first, count):
+            kv_bank = ring.tile([P, count, SLOTS, P], BF16, name="kv_bank", tag="ring")
+            for c in range(count):
+                for s in range(SLOTS):
+                    nc.tensor.transpose(kv_bank[:, c, s, :], kv_rows[:, first + c, s, :], ident_bf16[:])
+            nc.vector.tensor_copy(out=kv_t[:, first : first + count, :, :], in_=kv_bank[:])
+
+        def prepare_decay_and_bias():
             decay_bank = ring.tile([P, P], BF16, name="decay_bank", tag="ring")
             nc.tensor.transpose(decay_bank[:], decay_rows[:], ident_bf16[:])
             nc.vector.tensor_copy(out=decay_t[:], in_=decay_bank[:])
@@ -156,30 +156,34 @@ def tile_parallelretention_pb_kernel(tc, x, Wq, bq, kv, decay_mask, out):
             nc.tensor.matmul(out=bias_bank[:], lhsT=ones_bf16[:], rhs=bias_rows[:], start=True, stop=True)
             nc.vector.tensor_copy(out=bias_all[:], in_=bias_bank[:])
 
-        def transposes(g, c):
-            if live(g):
-                for j in range(CHUNK_SLOTS):
-                    word_banks[(g, c, j)] = transpose_words(x_rows[(g, c * CHUNK_SLOTS + j)][:].bitcast(F32))
+        def transposes(c):
+            if live(c):
+                for s in range(SLOTS):
+                    word_banks[(c, s)] = transpose_words(x_rows[(c, s)][:].bitcast(F32))
 
-        def pack(g, c, j):
-            if live(g):
+        def empty_banks(c, s):
+            if live(c):
+                grouped_tile[(c, s)] = regroup(word_banks[(c, s)])
+
+        def pack(c, s):
+            if live(c):
                 codes = mx_pool.tile([P, PASSES * P], U32, name="x_codes", align_bytes=64)
                 scales = mx_pool.tile([P, PASSES * P], U8, name="x_scales", align_bytes=64)
-                quantise(regroup(word_banks[(g, c, j)]), codes, scales)
-                x_mx[(g, c, j)] = (codes, scales)
+                quantise(grouped_tile[(c, s)], codes, scales)
+                x_mx[(c, s)] = (codes, scales)
 
-        def products(g, c):
-            if not live(g):
+        def products(c):
+            if not live(c):
                 return
-            qg_bank = qg_psum.tile([P, 2, CHUNK_SLOTS, P], F32, name="qg_bank")
-            q_bank[(g, c)] = qg_bank[:, 0, :, :]
-            g_bank[(g, c)] = qg_bank[:, 1, :, :]
-            for j in range(CHUNK_SLOTS):
-                codes, scales = x_mx[(g, c, j)]
+            qg_bank = qg_psum.tile([P, 2, SLOTS, P], F32, name="qg_bank")
+            q_bank[c] = qg_bank[:, 0, :, :]
+            g_bank[c] = qg_bank[:, 1, :, :]
+            for s in range(SLOTS):
+                codes, scales = x_mx[(c, s)]
                 for k_pass in range(PASSES):
                     cols = slice(k_pass * P, (k_pass + 1) * P)
                     nc.tensor.matmul_mx(
-                        out=q_bank[(g, c)][:, j, :],
+                        out=q_bank[c][:, s, :],
                         lhsT=codes[:, cols].bitcast(FP8X4),
                         lhsT_scale=scales[:, cols],
                         rhs=wq_codes[:, cols].bitcast(FP8X4),
@@ -187,91 +191,116 @@ def tile_parallelretention_pb_kernel(tc, x, Wq, bq, kv, decay_mask, out):
                         start=(k_pass == 0),
                         stop=(k_pass == PASSES - 1),
                     )
-            for j in range(CHUNK_SLOTS):
-                nc.tensor.matmul(
-                    out=g_bank[(g, c)][:, j, :], lhsT=kv_t[:, g, c * CHUNK_SLOTS + j, :], rhs=decay_t[:], start=True, stop=True
+            for s in range(SLOTS):
+                nc.tensor.matmul(out=g_bank[c][:, s, :], lhsT=kv_t[:, c, s, :], rhs=decay_t[:], start=True, stop=True)
+
+        def add_bias(c):
+            if live(c):
+                biased_tile[c] = work.tile([P, SLOTS, P], F32, name="biased")
+                nc.vector.tensor_tensor(
+                    out=biased_tile[c][:],
+                    in0=q_bank[c],
+                    in1=bias_all[:].unsqueeze(1).to_broadcast([P, SLOTS, P]),
+                    op=ALU.add,
                 )
 
-        def weigh(g, c):
-            if not live(g):
-                return
-            if c == 0:
-                y_tile[g] = work.tile([P, SLOTS, P], F32, name="y_tile")
-                row_sums[g] = small.tile([P, CHUNKS], F32, name="row_sums")
-            slots = slice(c * CHUNK_SLOTS, (c + 1) * CHUNK_SLOTS)
-            biased = work.tile([P, CHUNK_SLOTS, P], F32, name="biased")
-            nc.vector.tensor_tensor(
-                out=biased[:],
-                in0=q_bank[(g, c)],
-                in1=bias_all[:].unsqueeze(1).to_broadcast([P, CHUNK_SLOTS, P]),
-                op=ALU.add,
-            )
-            nc.vector.scalar_tensor_tensor(
-                out=y_tile[g][:, slots, :].rearrange("p s q -> p (s q)"),
-                in0=biased[:].rearrange("p s q -> p (s q)"),
-                scalar=1.0,
-                in1=g_bank[(g, c)].rearrange("p s q -> p (s q)"),
-                op0=ALU.mult,
-                op1=ALU.mult,
-                accum_out=row_sums[g][:, c : c + 1],
-            )
-
-        def mean_of(g):
-            if not live(g):
-                return
-            sums_bank[g] = sum_psum.tile([P, CHUNKS + 1], F32, name="sums_bank")
-            nc.tensor.matmul(out=sums_bank[g][:, 0:CHUNKS], lhsT=sample_mean[:], rhs=row_sums[g][:], start=True, stop=True)
-            mean_column[g] = small.tile([P, 1], F32, name="mean_column")
-            nc.vector.tensor_reduce(out=mean_column[g][:], in_=sums_bank[g][:, 0:CHUNKS], axis=mybir.AxisListType.X, op=ALU.add)
-
-        def squares(g):
-            if not live(g):
-                return
-            squared = work.tile([P, SLOTS * P], F32, name="squared")
-            square_sums[g] = small.tile([P, 1], F32, name="square_sums")
-            nc.scalar.activation(
-                out=squared[:],
-                in_=y_tile[g][:].rearrange("p s q -> p (s q)"),
-                func=ACT.Square,
-                bias=mean_column[g][:],
-                scale=-1.0,
-                accum_out=square_sums[g][:],
-            )
-
-        def variance_of(g):
-            if live(g):
-                nc.tensor.matmul(
-                    out=sums_bank[g][:, CHUNKS : CHUNKS + 1], lhsT=sample_mean[:], rhs=square_sums[g][:], start=True, stop=True
+        def weigh(c):
+            if live(c):
+                y_tile[c] = work.tile([P, SLOTS * P], F32, name="y_tile")
+                nc.vector.scalar_tensor_tensor(
+                    out=y_tile[c][:],
+                    in0=biased_tile[c][:].rearrange("p s q -> p (s q)"),
+                    scalar=1.0,
+                    in1=g_bank[c].rearrange("p s q -> p (s q)"),
+                    op0=ALU.mult,
+                    op1=ALU.mult,
+                    accum_out=row_sums[:, c : c + 1],
                 )
 
-        def finish(g):
-            if not live(g):
-                return
-            rstd = small.tile([P, 1], F32, name="rstd")
-            nc.scalar.activation(
-                out=rstd[:], in_=sums_bank[g][:, CHUNKS : CHUNKS + 1], func=ACT.Abs_reciprocal_sqrt, bias=eps_column[:]
-            )
-            res = work.tile([P, SLOTS, P], F32, name="res")
-            nc.vector.tensor_scalar(
-                out=res[:], in0=y_tile[g][:], scalar1=mean_column[g][:], scalar2=rstd[:], op0=ALU.subtract, op1=ALU.mult
-            )
-            nc.sync.dma_start(out=out_slots[g], in_=res[:])
+        def mean_of(first, count):
+            if live(first):
+                chunks = slice(first, first + count)
+                nc.tensor.matmul(out=sums_bank[:, 0, chunks], lhsT=sample_mean[:], rhs=row_sums[:, chunks], start=True, stop=True)
+                nc.scalar.copy(out=mean_columns[:, chunks], in_=sums_bank[:, 0, chunks])
 
-        for i in range(GROUPS + 2):
-            transposes(i, 0)
-            variance_of(i - 2)
-            products(i - 1, 1)
-            pack(i, 0, 0)
-            weigh(i - 1, 1)
-            pack(i, 0, 1)
-            finish(i - 2)
-            if i == 0:
-                prepare_kv()
+        def squares(c):
+            if live(c):
+                squared = work.tile([P, SLOTS * P], F32, name="squared")
+                nc.scalar.activation(
+                    out=squared[:],
+                    in_=y_tile[c][:],
+                    func=ACT.Square,
+                    bias=mean_columns[:, c : c + 1],
+                    scale=-1.0,
+                    accum_out=square_sums[:, c : c + 1],
+                )
 
-            transposes(i, 1)
-            mean_of(i - 1)
-            products(i, 0)
-            pack(i, 1, 0)
-            squares(i - 1)
-            weigh(i, 0)
-            pack(i, 1, 1)
+        def deviation_of(first, count):
+            if live(first):
+                chunks = slice(first, first + count)
+                nc.tensor.matmul(out=sums_bank[:, 1, chunks], lhsT=sample_mean[:], rhs=square_sums[:, chunks], start=True, stop=True)
+                nc.scalar.activation(
+                    out=rstd_columns[:, chunks], in_=sums_bank[:, 1, chunks], func=ACT.Abs_reciprocal_sqrt, bias=eps_column[:]
+                )
+
+        def finish(c):
+            if live(c):
+                res = work.tile([P, SLOTS, P], F32, name="res")
+                nc.vector.tensor_scalar(
+                    out=res[:].rearrange("p s q -> p (s q)"),
+                    in0=y_tile[c][:],
+                    scalar1=mean_columns[:, c : c + 1],
+                    scalar2=rstd_columns[:, c : c + 1],
+                    op0=ALU.subtract,
+                    op1=ALU.mult,
+                )
+                nc.sync.dma_start(out=out_slots[c], in_=res[:])
+
+        with tc.manual_schedule():
+            quantise(regroup(transpose_words(wq_rows[:].bitcast(F32))), wq_codes, wq_scales)
+
+            for i in range(CHUNKS):
+                transposes(i)
+                if i == 2:
+                    prepare_kv(0, CHUNKS // 2)
+                    prepare_decay_and_bias()
+                if i == 3:
+                    prepare_kv(CHUNKS // 2, CHUNKS // 2)
+                products(i - 2)
+                pack(i - 1, 1)
+                add_bias(i - 3)
+                empty_banks(i, 0)
+                if i == 7:
+                    finish(0)
+                    finish(1)
+                weigh(i - 3)
+                pack(i, 0)
+                empty_banks(i, 1)
+                if i == 5 or i == 7:
+                    mean_of(i - 5, 2)
+                    squares(i - 5)
+                    squares(i - 4)
+                if i == 6:
+                    deviation_of(0, 2)
+        last = CHUNKS - 1
+        add_bias(last - 2)
+        weigh(last - 2)
+        products(last - 1)
+        deviation_of(2, 2)
+        pack(last, 1)
+        products(last)
+        mean_of(4, 2)
+        squares(4)
+        squares(5)
+        deviation_of(4, 2)
+        add_bias(last - 1)
+        weigh(last - 1)
+        mean_of(last - 1, 1)
+        squares(last - 1)
+        add_bias(last)
+        weigh(last)
+        mean_of(last, 1)
+        squares(last)
+        deviation_of(last - 1, 2)
+        for c in range(2, CHUNKS):
+            finish(c)

@@ -24,7 +24,7 @@ CHUNKS = TOKENS // (P * SLOTS)
 SAMPLE_PARTITIONS = P // SLOTS
 SAMPLE_SIZE = 128 * 128
 EPS = 1e-5
-KV_AFTER = 2
+KV_AFTER = 0
 VECTOR_SHARE = 8
 
 FLOPS = 2 * TOKENS * E * P + 2 * TOKENS * P * P
@@ -39,6 +39,7 @@ def tile_parallelretention_pb_kernel(tc, x, Wq, bq, kv, decay_mask, out):
     with ExitStack() as ctx:
         const = ctx.enter_context(tc.tile_pool(name="const", bufs=1))
         x_pool = ctx.enter_context(tc.tile_pool(name="x_pool", bufs=CHUNKS * SLOTS))
+        split_pool = ctx.enter_context(tc.tile_pool(name="split_pool", bufs=6))
         grouped_pool = ctx.enter_context(tc.tile_pool(name="grouped_pool", bufs=4))
         mx_pool = ctx.enter_context(tc.tile_pool(name="mx_pool", bufs=8))
         work = ctx.enter_context(tc.tile_pool(name="work", bufs=CHUNKS))
@@ -87,13 +88,17 @@ def tile_parallelretention_pb_kernel(tc, x, Wq, bq, kv, decay_mask, out):
 
         banks_emptied = []
 
-        def transpose_words(words):
+        def transpose_words(words, split):
             banks = []
             for half in range(HALVES):
                 bank = ring.tile([P, BANK_PLANES, P], F32, name="word_bank", tag="ring")
                 for plane in range(BANK_PLANES):
                     k_pass, u = divmod(half * BANK_PLANES + plane, 2)
-                    pair_words = slice(k_pass * 2 * WORDS + u, (k_pass + 1) * 2 * WORDS, 2)
+                    first = k_pass * 2 * WORDS
+                    if split:
+                        pair_words = slice(first + u * WORDS, first + (u + 1) * WORDS)
+                    else:
+                        pair_words = slice(first + u, first + 2 * WORDS, 2)
                     nc.tensor.transpose(bank[:, plane, :], words[:, pair_words], ident_f32[:])
                 banks.append(bank)
             return banks
@@ -123,6 +128,7 @@ def tile_parallelretention_pb_kernel(tc, x, Wq, bq, kv, decay_mask, out):
         wq_scales = const.tile([P, PASSES * P], U8, align_bytes=64)
 
         word_banks = {}
+        x_split = {}
         grouped_tile = {}
         x_mx = {}
         q_bank = {}
@@ -142,24 +148,45 @@ def tile_parallelretention_pb_kernel(tc, x, Wq, bq, kv, decay_mask, out):
             return 0 <= c < CHUNKS
 
         def prepare_kv(first, count):
-            kv_bank = ring.tile([P, count, SLOTS, P], BF16, name="kv_bank", tag="ring")
+            kv_bank = qg_psum.tile([P, count, SLOTS, P], BF16, name="kv_bank", tag="qg")
             for c in range(count):
                 for s in range(SLOTS):
                     nc.tensor.transpose(kv_bank[:, c, s, :], kv_rows[:, first + c, s, :], ident_bf16[:])
             nc.vector.tensor_copy(out=kv_t[:, first : first + count, :, :], in_=kv_bank[:])
 
-        def prepare_decay_and_bias():
-            decay_bank = ring.tile([P, P], BF16, name="decay_bank", tag="ring")
+        def prepare_decay():
+            decay_bank = qg_psum.tile([P, P], BF16, name="decay_bank", tag="qg")
             nc.tensor.transpose(decay_bank[:], decay_rows[:], ident_bf16[:])
             nc.vector.tensor_copy(out=decay_t[:], in_=decay_bank[:])
-            bias_bank = ring.tile([P, P], F32, name="bias_bank", tag="ring")
+
+        def prepare_bias():
+            bias_bank = qg_psum.tile([P, P], F32, name="bias_bank", tag="qg")
             nc.tensor.matmul(out=bias_bank[:], lhsT=ones_bf16[:], rhs=bias_rows[:], start=True, stop=True)
             nc.vector.tensor_copy(out=bias_all[:], in_=bias_bank[:])
 
         def transposes(c):
             if live(c):
                 for s in range(SLOTS):
-                    word_banks[(c, s)] = transpose_words(x_rows[(c, s)][:].bitcast(F32))
+                    split = (c, s) in x_split
+                    rows = x_split[(c, s)] if split else x_rows[(c, s)]
+                    word_banks[(c, s)] = transpose_words(rows[:].bitcast(F32), split)
+
+        def split_words(c, s, engine):
+            if live(c):
+                rows = split_pool.tile([P, E], BF16, name="x_split")
+                if engine is nc.gpsimd:
+                    for k_pass in range(PASSES):
+                        columns = slice(k_pass * P * PACK, (k_pass + 1) * P * PACK)
+                        engine.tensor_copy(
+                            out=rows[:, columns].bitcast(U32).rearrange("p (u w) -> p u w", u=2),
+                            in_=x_rows[(c, s)][:, columns].bitcast(U32).rearrange("p (w u) -> p u w", u=2),
+                        )
+                else:
+                    engine.tensor_copy(
+                        out=rows[:].bitcast(F32).rearrange("p (g u w) -> p g u w", g=PASSES, u=2),
+                        in_=x_rows[(c, s)][:].bitcast(F32).rearrange("p (g w u) -> p g u w", g=PASSES, u=2),
+                    )
+                x_split[(c, s)] = rows
 
         def empty_banks(c, s):
             if live(c):
@@ -175,7 +202,7 @@ def tile_parallelretention_pb_kernel(tc, x, Wq, bq, kv, decay_mask, out):
         def products(c):
             if not live(c):
                 return
-            qg_bank = qg_psum.tile([P, 2, SLOTS, P], F32, name="qg_bank")
+            qg_bank = qg_psum.tile([P, 2, SLOTS, P], F32, name="qg_bank", tag="qg")
             q_bank[c] = qg_bank[:, 0, :, :]
             g_bank[c] = qg_bank[:, 1, :, :]
             for s in range(SLOTS):
@@ -257,18 +284,16 @@ def tile_parallelretention_pb_kernel(tc, x, Wq, bq, kv, decay_mask, out):
                 nc.sync.dma_start(out=out_slots[c], in_=res[:])
 
         with tc.manual_schedule():
-            quantise(regroup(transpose_words(wq_rows[:].bitcast(F32))), wq_codes, wq_scales)
+            quantise(regroup(transpose_words(wq_rows[:].bitcast(F32), False)), wq_codes, wq_scales)
 
             for i in range(CHUNKS):
                 transposes(i)
-                if i == 2:
-                    prepare_kv(0, CHUNKS // 2)
-                    prepare_decay_and_bias()
-                if i == 3:
-                    prepare_kv(CHUNKS // 2, CHUNKS // 2)
                 products(i - 2)
                 pack(i - 1, 1)
                 add_bias(i - 3)
+                split_words(i + 1, 0, nc.vector)
+                if i % 2 == 0:
+                    split_words(i + 1, 1, nc.gpsimd)
                 empty_banks(i, 0)
                 if i == 7:
                     finish(0)
@@ -276,6 +301,11 @@ def tile_parallelretention_pb_kernel(tc, x, Wq, bq, kv, decay_mask, out):
                 weigh(i - 3)
                 pack(i, 0)
                 empty_banks(i, 1)
+                if i == 0:
+                    prepare_kv(0, CHUNKS // 2)
+                    prepare_kv(CHUNKS // 2, CHUNKS // 2)
+                    prepare_decay()
+                    prepare_bias()
                 if i == 5 or i == 7:
                     mean_of(i - 5, 2)
                     squares(i - 5)
@@ -292,11 +322,11 @@ def tile_parallelretention_pb_kernel(tc, x, Wq, bq, kv, decay_mask, out):
         mean_of(4, 2)
         squares(4)
         squares(5)
-        deviation_of(4, 2)
         add_bias(last - 1)
         weigh(last - 1)
         mean_of(last - 1, 1)
         squares(last - 1)
+        deviation_of(4, 2)
         add_bias(last)
         weigh(last)
         mean_of(last, 1)

@@ -25,7 +25,7 @@ SAMPLE_PARTITIONS = P // SLOTS
 SAMPLE_SIZE = 128 * 128
 EPS = 1e-5
 KV_AFTER = 0
-VECTOR_SHARE = 8
+VECTOR_SHARE = 34
 
 FLOPS = 2 * TOKENS * E * P + 2 * TOKENS * P * P
 
@@ -111,7 +111,7 @@ def tile_parallelretention_pb_kernel(tc, x, Wq, bq, kv, decay_mask, out):
                 side_by_side = grouped[:].bitcast(F32)[:, first : first + passes_per_bank, :, :]
                 planes = banks[half][:].rearrange("p (g u) r -> p g r u", u=PACK // 2)
                 banks_emptied.append(half)
-                if len(banks_emptied) % VECTOR_SHARE == 2:
+                if len(banks_emptied) % VECTOR_SHARE == 0:
                     nc.vector.tensor_copy(out=side_by_side, in_=planes)
                 else:
                     nc.scalar.copy(out=side_by_side, in_=planes)
@@ -171,21 +171,13 @@ def tile_parallelretention_pb_kernel(tc, x, Wq, bq, kv, decay_mask, out):
                     rows = x_split[(c, s)] if split else x_rows[(c, s)]
                     word_banks[(c, s)] = transpose_words(rows[:].bitcast(F32), split)
 
-        def split_words(c, s, engine):
+        def split_words(c, s):
             if live(c):
                 rows = split_pool.tile([P, E], BF16, name="x_split")
-                if engine is nc.gpsimd:
-                    for k_pass in range(PASSES):
-                        columns = slice(k_pass * P * PACK, (k_pass + 1) * P * PACK)
-                        engine.tensor_copy(
-                            out=rows[:, columns].bitcast(U32).rearrange("p (u w) -> p u w", u=2),
-                            in_=x_rows[(c, s)][:, columns].bitcast(U32).rearrange("p (w u) -> p u w", u=2),
-                        )
-                else:
-                    engine.tensor_copy(
-                        out=rows[:].bitcast(F32).rearrange("p (g u w) -> p g u w", g=PASSES, u=2),
-                        in_=x_rows[(c, s)][:].bitcast(F32).rearrange("p (g w u) -> p g u w", g=PASSES, u=2),
-                    )
+                nc.vector.tensor_copy(
+                    out=rows[:].bitcast(F32).rearrange("p (g u w) -> p g u w", g=PASSES, u=2),
+                    in_=x_rows[(c, s)][:].bitcast(F32).rearrange("p (g w u) -> p g u w", g=PASSES, u=2),
+                )
                 x_split[(c, s)] = rows
 
         def empty_banks(c, s):
@@ -291,9 +283,7 @@ def tile_parallelretention_pb_kernel(tc, x, Wq, bq, kv, decay_mask, out):
                 products(i - 2)
                 pack(i - 1, 1)
                 add_bias(i - 3)
-                split_words(i + 1, 0, nc.vector)
-                if i % 2 == 0:
-                    split_words(i + 1, 1, nc.gpsimd)
+                split_words(i + 1, 0)
                 empty_banks(i, 0)
                 if i == 7:
                     finish(0)

@@ -25,7 +25,8 @@ SAMPLE_PARTITIONS = P // SLOTS
 SAMPLE_SIZE = 128 * 128
 EPS = 1e-5
 KV_AFTER = 0
-VECTOR_SHARE = 34
+
+SPLIT_FROM = 3
 
 FLOPS = 2 * TOKENS * E * P + 2 * TOKENS * P * P
 
@@ -86,8 +87,6 @@ def tile_parallelretention_pb_kernel(tc, x, Wq, bq, kv, decay_mask, out):
         table_warmer = const.tile([P, 1], F32)
         nc.scalar.activation(out=table_warmer[:], in_=eps_column[:], func=ACT.Abs_reciprocal_sqrt)
 
-        banks_emptied = []
-
         def transpose_words(words, split):
             banks = []
             for half in range(HALVES):
@@ -110,11 +109,7 @@ def tile_parallelretention_pb_kernel(tc, x, Wq, bq, kv, decay_mask, out):
                 first = half * passes_per_bank
                 side_by_side = grouped[:].bitcast(F32)[:, first : first + passes_per_bank, :, :]
                 planes = banks[half][:].rearrange("p (g u) r -> p g r u", u=PACK // 2)
-                banks_emptied.append(half)
-                if len(banks_emptied) % VECTOR_SHARE == 0:
-                    nc.vector.tensor_copy(out=side_by_side, in_=planes)
-                else:
-                    nc.scalar.copy(out=side_by_side, in_=planes)
+                nc.scalar.copy(out=side_by_side, in_=planes)
             return grouped
 
         def quantise(grouped, codes, scales):
@@ -280,47 +275,46 @@ def tile_parallelretention_pb_kernel(tc, x, Wq, bq, kv, decay_mask, out):
 
             for i in range(CHUNKS):
                 transposes(i)
+                if i == 1:
+                    prepare_decay()
+                    prepare_bias()
                 products(i - 2)
                 pack(i - 1, 1)
                 add_bias(i - 3)
-                split_words(i + 1, 0)
+                if i + 1 >= SPLIT_FROM:
+                    split_words(i + 1, 0)
                 empty_banks(i, 0)
-                if i == 7:
-                    finish(0)
-                    finish(1)
                 weigh(i - 3)
                 pack(i, 0)
                 empty_banks(i, 1)
                 if i == 0:
                     prepare_kv(0, CHUNKS // 2)
                     prepare_kv(CHUNKS // 2, CHUNKS // 2)
-                    prepare_decay()
-                    prepare_bias()
                 if i == 5 or i == 7:
                     mean_of(i - 5, 2)
                     squares(i - 5)
                     squares(i - 4)
                 if i == 6:
                     deviation_of(0, 2)
-        last = CHUNKS - 1
-        add_bias(last - 2)
-        weigh(last - 2)
-        products(last - 1)
-        deviation_of(2, 2)
-        pack(last, 1)
-        products(last)
-        mean_of(4, 2)
-        squares(4)
-        squares(5)
-        add_bias(last - 1)
-        weigh(last - 1)
-        mean_of(last - 1, 1)
-        squares(last - 1)
-        deviation_of(4, 2)
-        add_bias(last)
-        weigh(last)
-        mean_of(last, 1)
-        squares(last)
-        deviation_of(last - 1, 2)
-        for c in range(2, CHUNKS):
-            finish(c)
+            last = CHUNKS - 1
+            add_bias(last - 2)
+            products(last - 1)
+            weigh(last - 2)
+            pack(last, 1)
+            mean_of(last - 3, 2)
+            products(last)
+            deviation_of(last - 5, 2)
+            add_bias(last - 1)
+            squares(last - 3)
+            weigh(last - 1)
+            squares(last - 2)
+            mean_of(last - 1, 1)
+            add_bias(last)
+            squares(last - 1)
+            weigh(last)
+            mean_of(last, 1)
+            deviation_of(last - 3, 2)
+            squares(last)
+            deviation_of(last - 1, 2)
+            for c in range(CHUNKS):
+                finish(c)

@@ -26,7 +26,7 @@ SAMPLE_SIZE = 128 * 128
 EPS = 1e-5
 KV_AFTER = 0
 
-SPLIT_FROM = 3
+SPLIT = range(3, 7)
 
 FLOPS = 2 * TOKENS * E * P + 2 * TOKENS * P * P
 
@@ -44,7 +44,7 @@ def tile_parallelretention_pb_kernel(tc, x, Wq, bq, kv, decay_mask, out):
         grouped_pool = ctx.enter_context(tc.tile_pool(name="grouped_pool", bufs=4))
         mx_pool = ctx.enter_context(tc.tile_pool(name="mx_pool", bufs=8))
         work = ctx.enter_context(tc.tile_pool(name="work", bufs=CHUNKS))
-        ring = ctx.enter_context(tc.psum_pool(name="ring", bufs=5))
+        ring = ctx.enter_context(tc.psum_pool(name="ring", bufs=4))
         qg_psum = ctx.enter_context(tc.psum_pool(name="qg_psum", bufs=2))
         sum_psum = ctx.enter_context(tc.psum_pool(name="sum_psum", bufs=1))
 
@@ -135,7 +135,8 @@ def tile_parallelretention_pb_kernel(tc, x, Wq, bq, kv, decay_mask, out):
         mean_columns = const.tile([P, CHUNKS], F32)
         square_sums = const.tile([P, CHUNKS], F32)
         rstd_columns = const.tile([P, CHUNKS], F32)
-        sums_bank = sum_psum.tile([P, 2, CHUNKS], F32, name="sums_bank")
+        means_bank = sum_psum.tile([P, CHUNKS], F32, name="means_bank")
+        variances_bank = sum_psum.tile([P, CHUNKS], F32, name="variances_bank")
         decay_t = const.tile([P, P], BF16)
         bias_all = const.tile([P, P], F32)
 
@@ -193,6 +194,8 @@ def tile_parallelretention_pb_kernel(tc, x, Wq, bq, kv, decay_mask, out):
             q_bank[c] = qg_bank[:, 0, :, :]
             g_bank[c] = qg_bank[:, 1, :, :]
             for s in range(SLOTS):
+                nc.tensor.matmul(out=g_bank[c][:, s, :], lhsT=kv_t[:, c, s, :], rhs=decay_t[:], start=True, stop=True)
+            for s in range(SLOTS):
                 codes, scales = x_mx[(c, s)]
                 for k_pass in range(PASSES):
                     cols = slice(k_pass * P, (k_pass + 1) * P)
@@ -205,8 +208,6 @@ def tile_parallelretention_pb_kernel(tc, x, Wq, bq, kv, decay_mask, out):
                         start=(k_pass == 0),
                         stop=(k_pass == PASSES - 1),
                     )
-            for s in range(SLOTS):
-                nc.tensor.matmul(out=g_bank[c][:, s, :], lhsT=kv_t[:, c, s, :], rhs=decay_t[:], start=True, stop=True)
 
         def add_bias(c):
             if live(c):
@@ -234,8 +235,8 @@ def tile_parallelretention_pb_kernel(tc, x, Wq, bq, kv, decay_mask, out):
         def mean_of(first, count):
             if live(first):
                 chunks = slice(first, first + count)
-                nc.tensor.matmul(out=sums_bank[:, 0, chunks], lhsT=sample_mean[:], rhs=row_sums[:, chunks], start=True, stop=True)
-                nc.scalar.copy(out=mean_columns[:, chunks], in_=sums_bank[:, 0, chunks])
+                nc.tensor.matmul(out=means_bank[:, chunks], lhsT=sample_mean[:], rhs=row_sums[:, chunks], start=True, stop=True)
+                nc.scalar.copy(out=mean_columns[:, chunks], in_=means_bank[:, chunks])
 
         def squares(c):
             if live(c):
@@ -252,9 +253,9 @@ def tile_parallelretention_pb_kernel(tc, x, Wq, bq, kv, decay_mask, out):
         def deviation_of(first, count):
             if live(first):
                 chunks = slice(first, first + count)
-                nc.tensor.matmul(out=sums_bank[:, 1, chunks], lhsT=sample_mean[:], rhs=square_sums[:, chunks], start=True, stop=True)
+                nc.tensor.matmul(out=variances_bank[:, chunks], lhsT=sample_mean[:], rhs=square_sums[:, chunks], start=True, stop=True)
                 nc.scalar.activation(
-                    out=rstd_columns[:, chunks], in_=sums_bank[:, 1, chunks], func=ACT.Abs_reciprocal_sqrt, bias=eps_column[:]
+                    out=rstd_columns[:, chunks], in_=variances_bank[:, chunks], func=ACT.Abs_reciprocal_sqrt, bias=eps_column[:]
                 )
 
         def finish(c):
@@ -281,7 +282,7 @@ def tile_parallelretention_pb_kernel(tc, x, Wq, bq, kv, decay_mask, out):
                 products(i - 2)
                 pack(i - 1, 1)
                 add_bias(i - 3)
-                if i + 1 >= SPLIT_FROM:
+                if i + 1 in SPLIT:
                     split_words(i + 1, 0)
                 empty_banks(i, 0)
                 weigh(i - 3)
@@ -311,10 +312,11 @@ def tile_parallelretention_pb_kernel(tc, x, Wq, bq, kv, decay_mask, out):
             mean_of(last - 1, 1)
             add_bias(last)
             squares(last - 1)
+            deviation_of(last - 3, 2)
+            finish(0)
             weigh(last)
             mean_of(last, 1)
-            deviation_of(last - 3, 2)
             squares(last)
             deviation_of(last - 1, 2)
-            for c in range(CHUNKS):
+            for c in range(1, CHUNKS):
                 finish(c)

@@ -21,6 +21,7 @@ BANK_PLANES = 4
 HALVES = E // 2 // (WORDS * BANK_PLANES)
 SLOTS = 2
 CHUNKS = TOKENS // (P * SLOTS)
+KV_RUN = TOKENS // P // SLOTS
 SAMPLE_PARTITIONS = P // SLOTS
 SAMPLE_SIZE = 128 * 128
 EPS = 1e-5
@@ -34,7 +35,7 @@ FLOPS = 2 * TOKENS * E * P + 2 * TOKENS * P * P
 def tile_parallelretention_pb_kernel(tc, x, Wq, bq, kv, decay_mask, out):
     nc = tc.nc
     x_slots = x.flatten_outer_dims().rearrange("(c p s) k -> c p s k", p=P, s=SLOTS)
-    kv_slots = kv.flatten_outer_dims().rearrange("(c p s) k -> p c s k", p=P, s=SLOTS)
+    kv_runs = kv.flatten_outer_dims().rearrange("(p j s) k -> p j s k", p=P, s=SLOTS)
     out_slots = out.flatten_outer_dims().rearrange("(c p s) q -> c p s q", p=P, s=SLOTS)
 
     with ExitStack() as ctx:
@@ -44,14 +45,14 @@ def tile_parallelretention_pb_kernel(tc, x, Wq, bq, kv, decay_mask, out):
         grouped_pool = ctx.enter_context(tc.tile_pool(name="grouped_pool", bufs=4))
         mx_pool = ctx.enter_context(tc.tile_pool(name="mx_pool", bufs=8))
         work = ctx.enter_context(tc.tile_pool(name="work", bufs=CHUNKS))
-        ring = ctx.enter_context(tc.psum_pool(name="ring", bufs=4))
+        ring = ctx.enter_context(tc.psum_pool(name="ring", bufs=5))
         qg_psum = ctx.enter_context(tc.psum_pool(name="qg_psum", bufs=2))
         sum_psum = ctx.enter_context(tc.psum_pool(name="sum_psum", bufs=1))
 
         wq_rows = const.tile([P, E], BF16)
         decay_rows = const.tile([P, P], BF16)
         bias_rows = const.tile([P, P], BF16)
-        kv_rows = const.tile([P, CHUNKS, SLOTS, P], BF16)
+        kv_rows = const.tile([P, KV_RUN, SLOTS, P], BF16)
         x_rows = {}
 
         def load_token_tile(c, s):
@@ -69,7 +70,7 @@ def tile_parallelretention_pb_kernel(tc, x, Wq, bq, kv, decay_mask, out):
             if c == KV_AFTER:
                 nc.sync.dma_start(out=decay_rows[:], in_=decay_mask.flatten_outer_dims())
                 nc.sync.dma_start(out=bias_rows[0:1, :], in_=bq.unsqueeze(0))
-                nc.sync.dma_start(out=kv_rows[:], in_=kv_slots)
+                nc.sync.dma_start(out=kv_rows[:], in_=kv_runs)
 
         ident_f32 = const.tile([P, P], F32)
         make_identity(nc, ident_f32[:])
@@ -130,25 +131,26 @@ def tile_parallelretention_pb_kernel(tc, x, Wq, bq, kv, decay_mask, out):
         g_bank = {}
         biased_tile = {}
         y_tile = {}
-        kv_t = const.tile([P, CHUNKS, SLOTS, P], BF16)
+        kv_t = const.tile([P, SLOTS, CHUNKS, P], BF16)
         row_sums = const.tile([P, CHUNKS], F32)
         mean_columns = const.tile([P, CHUNKS], F32)
         square_sums = const.tile([P, CHUNKS], F32)
         rstd_columns = const.tile([P, CHUNKS], F32)
-        means_bank = sum_psum.tile([P, CHUNKS], F32, name="means_bank")
-        variances_bank = sum_psum.tile([P, CHUNKS], F32, name="variances_bank")
+        sums_bank = sum_psum.tile([P, 2, CHUNKS], F32, name="sums_bank")
         decay_t = const.tile([P, P], BF16)
         bias_all = const.tile([P, P], F32)
 
         def live(c):
             return 0 <= c < CHUNKS
 
-        def prepare_kv(first, count):
-            kv_bank = qg_psum.tile([P, count, SLOTS, P], BF16, name="kv_bank", tag="qg")
-            for c in range(count):
-                for s in range(SLOTS):
-                    nc.tensor.transpose(kv_bank[:, c, s, :], kv_rows[:, first + c, s, :], ident_bf16[:])
-            nc.vector.tensor_copy(out=kv_t[:, first : first + count, :, :], in_=kv_bank[:])
+        def prepare_kv(s):
+            kv_bank = qg_psum.tile([P, KV_RUN, P], BF16, name="kv_bank", tag="qg")
+            for j in range(KV_RUN):
+                nc.tensor.transpose(kv_bank[:, j, :], kv_rows[:, j, s, :], ident_bf16[:])
+            nc.vector.tensor_copy(
+                out=kv_t[:, s, :, :].rearrange("p c (q j) -> p (c q) j", j=KV_RUN),
+                in_=kv_bank[:].rearrange("p j q -> p q j"),
+            )
 
         def prepare_decay():
             decay_bank = qg_psum.tile([P, P], BF16, name="decay_bank", tag="qg")
@@ -194,7 +196,7 @@ def tile_parallelretention_pb_kernel(tc, x, Wq, bq, kv, decay_mask, out):
             q_bank[c] = qg_bank[:, 0, :, :]
             g_bank[c] = qg_bank[:, 1, :, :]
             for s in range(SLOTS):
-                nc.tensor.matmul(out=g_bank[c][:, s, :], lhsT=kv_t[:, c, s, :], rhs=decay_t[:], start=True, stop=True)
+                nc.tensor.matmul(out=g_bank[c][:, s, :], lhsT=kv_t[:, s, c, :], rhs=decay_t[:], start=True, stop=True)
             for s in range(SLOTS):
                 codes, scales = x_mx[(c, s)]
                 for k_pass in range(PASSES):
@@ -235,8 +237,8 @@ def tile_parallelretention_pb_kernel(tc, x, Wq, bq, kv, decay_mask, out):
         def mean_of(first, count):
             if live(first):
                 chunks = slice(first, first + count)
-                nc.tensor.matmul(out=means_bank[:, chunks], lhsT=sample_mean[:], rhs=row_sums[:, chunks], start=True, stop=True)
-                nc.scalar.copy(out=mean_columns[:, chunks], in_=means_bank[:, chunks])
+                nc.tensor.matmul(out=sums_bank[:, 0, chunks], lhsT=sample_mean[:], rhs=row_sums[:, chunks], start=True, stop=True)
+                nc.scalar.copy(out=mean_columns[:, chunks], in_=sums_bank[:, 0, chunks])
 
         def squares(c):
             if live(c):
@@ -250,12 +252,12 @@ def tile_parallelretention_pb_kernel(tc, x, Wq, bq, kv, decay_mask, out):
                     accum_out=square_sums[:, c : c + 1],
                 )
 
-        def deviation_of(first, count):
+        def deviation_of(first, count, bank):
             if live(first):
                 chunks = slice(first, first + count)
-                nc.tensor.matmul(out=variances_bank[:, chunks], lhsT=sample_mean[:], rhs=square_sums[:, chunks], start=True, stop=True)
+                nc.tensor.matmul(out=bank[:, chunks], lhsT=sample_mean[:], rhs=square_sums[:, chunks], start=True, stop=True)
                 nc.scalar.activation(
-                    out=rstd_columns[:, chunks], in_=variances_bank[:, chunks], func=ACT.Abs_reciprocal_sqrt, bias=eps_column[:]
+                    out=rstd_columns[:, chunks], in_=bank[:, chunks], func=ACT.Abs_reciprocal_sqrt, bias=eps_column[:]
                 )
 
         def finish(c):
@@ -289,22 +291,23 @@ def tile_parallelretention_pb_kernel(tc, x, Wq, bq, kv, decay_mask, out):
                 pack(i, 0)
                 empty_banks(i, 1)
                 if i == 0:
-                    prepare_kv(0, CHUNKS // 2)
-                    prepare_kv(CHUNKS // 2, CHUNKS // 2)
+                    prepare_kv(0)
+                    prepare_kv(1)
                 if i == 5 or i == 7:
                     mean_of(i - 5, 2)
                     squares(i - 5)
                     squares(i - 4)
                 if i == 6:
-                    deviation_of(0, 2)
+                    deviation_of(0, 2, sums_bank[:, 1, :])
             last = CHUNKS - 1
+            late_bank = ring.tile([P, CHUNKS], F32, name="late_bank", tag="ring")
             add_bias(last - 2)
             products(last - 1)
             weigh(last - 2)
             pack(last, 1)
             mean_of(last - 3, 2)
             products(last)
-            deviation_of(last - 5, 2)
+            deviation_of(last - 5, 2, late_bank)
             add_bias(last - 1)
             squares(last - 3)
             weigh(last - 1)
@@ -312,11 +315,11 @@ def tile_parallelretention_pb_kernel(tc, x, Wq, bq, kv, decay_mask, out):
             mean_of(last - 1, 1)
             add_bias(last)
             squares(last - 1)
-            deviation_of(last - 3, 2)
+            deviation_of(last - 3, 2, late_bank)
             finish(0)
             weigh(last)
             mean_of(last, 1)
             squares(last)
-            deviation_of(last - 1, 2)
+            deviation_of(last - 1, 2, late_bank)
             for c in range(1, CHUNKS):
                 finish(c)

@@ -61,6 +61,8 @@ def tile_parallelretention_pb_kernel(tc, x, Wq, bq, kv, decay_mask, out):
             x_rows[(c, s)] = rows
 
         nc.vector.memset(bias_rows[:], 0.0)
+        nc.scalar.dma_start(out=decay_rows[:], in_=decay_mask.flatten_outer_dims())
+        nc.scalar.dma_start(out=bias_rows[0:1, :], in_=bq.unsqueeze(0))
         for half in range(HALVES):
             columns = slice(half * E // HALVES, (half + 1) * E // HALVES)
             nc.sync.dma_start(out=wq_rows[:, columns], in_=Wq[:, columns])
@@ -68,8 +70,6 @@ def tile_parallelretention_pb_kernel(tc, x, Wq, bq, kv, decay_mask, out):
             for s in range(SLOTS):
                 load_token_tile(c, s)
             if c == KV_AFTER:
-                nc.sync.dma_start(out=decay_rows[:], in_=decay_mask.flatten_outer_dims())
-                nc.sync.dma_start(out=bias_rows[0:1, :], in_=bq.unsqueeze(0))
                 nc.sync.dma_start(out=kv_rows[:], in_=kv_runs)
 
         ident_f32 = const.tile([P, P], F32)
@@ -282,8 +282,8 @@ def tile_parallelretention_pb_kernel(tc, x, Wq, bq, kv, decay_mask, out):
                     prepare_decay()
                     prepare_bias()
                 products(i - 2)
-                pack(i - 1, 1)
                 add_bias(i - 3)
+                pack(i - 1, 1)
                 if i + 1 in SPLIT:
                     split_words(i + 1, 0)
                 empty_banks(i, 0)
@@ -303,23 +303,25 @@ def tile_parallelretention_pb_kernel(tc, x, Wq, bq, kv, decay_mask, out):
             late_bank = ring.tile([P, CHUNKS], F32, name="late_bank", tag="ring")
             add_bias(last - 2)
             products(last - 1)
+            finish(0)
             weigh(last - 2)
+            deviation_of(last - 5, 2, late_bank)
             pack(last, 1)
             mean_of(last - 3, 2)
             products(last)
-            deviation_of(last - 5, 2, late_bank)
             add_bias(last - 1)
             squares(last - 3)
+            finish(1)
             weigh(last - 1)
             squares(last - 2)
             mean_of(last - 1, 1)
             add_bias(last)
             squares(last - 1)
             deviation_of(last - 3, 2, late_bank)
-            finish(0)
+            finish(2)
             weigh(last)
             mean_of(last, 1)
             squares(last)
             deviation_of(last - 1, 2, late_bank)
-            for c in range(1, CHUNKS):
+            for c in range(3, CHUNKS):
                 finish(c)

@@ -192,7 +192,8 @@ def tile_parallelretention_pb_kernel(tc, x, Wq, bq, kv, decay_mask, out):
         def products(c):
             if not live(c):
                 return
-            qg_bank = qg_psum.tile([P, 2, SLOTS, P], F32, name="qg_bank", tag="qg")
+            pool, tag = (ring, "ring") if c == CHUNKS - 1 else (qg_psum, "qg")
+            qg_bank = pool.tile([P, 2, SLOTS, P], F32, name="qg_bank", tag=tag)
             q_bank[c] = qg_bank[:, 0, :, :]
             g_bank[c] = qg_bank[:, 1, :, :]
             for s in range(SLOTS):
@@ -301,27 +302,27 @@ def tile_parallelretention_pb_kernel(tc, x, Wq, bq, kv, decay_mask, out):
                     deviation_of(0, 2, sums_bank[:, 1, :])
             last = CHUNKS - 1
             late_bank = ring.tile([P, CHUNKS], F32, name="late_bank", tag="ring")
-            add_bias(last - 2)
-            products(last - 1)
             finish(0)
-            weigh(last - 2)
-            deviation_of(last - 5, 2, late_bank)
-            pack(last, 1)
-            mean_of(last - 3, 2)
-            products(last)
-            add_bias(last - 1)
-            squares(last - 3)
+            products(last - 1)
             finish(1)
+            mean_of(last - 3, 1)
+            pack(last, 1)
+            products(last)
+            squares(last - 3)
+            add_bias(last - 2)
+            deviation_of(last - 5, 2, late_bank)
+            add_bias(last - 1)
+            weigh(last - 2)
             weigh(last - 1)
+            mean_of(last - 2, 2)
             squares(last - 2)
-            mean_of(last - 1, 1)
             add_bias(last)
             squares(last - 1)
-            deviation_of(last - 3, 2, late_bank)
             finish(2)
             weigh(last)
             mean_of(last, 1)
             squares(last)
-            deviation_of(last - 1, 2, late_bank)
+            deviation_of(last - 3, 3, late_bank)
+            deviation_of(last, 1, sums_bank[:, 1, :])
             for c in range(3, CHUNKS):
                 finish(c)

from contextlib import ExitStack

import concourse.mybir as mybir
from concourse.masks import make_identity

F32 = mybir.dt.float32
BF16 = mybir.dt.bfloat16
U32 = mybir.dt.uint32
U8 = mybir.dt.uint8
FP8X4 = mybir.dt.float8_e4m3fn_x4
ALU = mybir.AluOpType
ACT = mybir.ActivationFunctionType

P = 128
TOKENS = 16 * 128
E = 2048
PACK = 4
PASSES = E // (P * PACK)
WORDS = P
BANK_PLANES = 4
HALVES = E // 2 // (WORDS * BANK_PLANES)
SLOTS = 2
CHUNKS = TOKENS // (P * SLOTS)
KV_RUN = TOKENS // P // SLOTS
SAMPLE_PARTITIONS = P // SLOTS
SAMPLE_SIZE = 128 * 128
EPS = 1e-5
KV_AFTER = 0

SPLIT = range(3, 7)

FLOPS = 2 * TOKENS * E * P + 2 * TOKENS * P * P


def tile_parallelretention_pb_kernel(tc, x, Wq, bq, kv, decay_mask, out):
    nc = tc.nc
    x_slots = x.flatten_outer_dims().rearrange("(c p s) k -> c p s k", p=P, s=SLOTS)
    kv_runs = kv.flatten_outer_dims().rearrange("(p j s) k -> p j s k", p=P, s=SLOTS)
    out_slots = out.flatten_outer_dims().rearrange("(c p s) q -> c p s q", p=P, s=SLOTS)

    with ExitStack() as ctx:
        const = ctx.enter_context(tc.tile_pool(name="const", bufs=1))
        x_pool = ctx.enter_context(tc.tile_pool(name="x_pool", bufs=CHUNKS * SLOTS))
        split_pool = ctx.enter_context(tc.tile_pool(name="split_pool", bufs=6))
        grouped_pool = ctx.enter_context(tc.tile_pool(name="grouped_pool", bufs=4))
        mx_pool = ctx.enter_context(tc.tile_pool(name="mx_pool", bufs=8))
        work = ctx.enter_context(tc.tile_pool(name="work", bufs=CHUNKS))
        ring = ctx.enter_context(tc.psum_pool(name="ring", bufs=5))
        qg_psum = ctx.enter_context(tc.psum_pool(name="qg_psum", bufs=2))
        sum_psum = ctx.enter_context(tc.psum_pool(name="sum_psum", bufs=1))

        wq_rows = const.tile([P, E], BF16)
        decay_rows = const.tile([P, P], BF16)
        bias_rows = const.tile([P, P], BF16)
        kv_rows = const.tile([P, KV_RUN, SLOTS, P], BF16)
        x_rows = {}

        def load_token_tile(c, s):
            rows = x_pool.tile([P, E], BF16, name="x_tile")
            nc.sync.dma_start(out=rows[:], in_=x_slots[c][:, s, :])
            x_rows[(c, s)] = rows

        nc.vector.memset(bias_rows[:], 0.0)
        nc.scalar.dma_start(out=decay_rows[:], in_=decay_mask.flatten_outer_dims())
        nc.scalar.dma_start(out=bias_rows[0:1, :], in_=bq.unsqueeze(0))
        for half in range(HALVES):
            columns = slice(half * E // HALVES, (half + 1) * E // HALVES)
            nc.sync.dma_start(out=wq_rows[:, columns], in_=Wq[:, columns])
        for c in range(CHUNKS):
            for s in range(SLOTS):
                load_token_tile(c, s)
            if c == KV_AFTER:
                nc.sync.dma_start(out=kv_rows[:], in_=kv_runs)

        ident_f32 = const.tile([P, P], F32)
        make_identity(nc, ident_f32[:])
        ident_bf16 = const.tile([P, P], BF16)
        make_identity(nc, ident_bf16[:])
        ones_bf16 = const.tile([P, P], BF16)
        nc.vector.memset(ones_bf16[:], 1.0)
        eps_column = const.tile([P, 1], F32)
        nc.vector.memset(eps_column[:], EPS)
        sample_mean = const.tile([P, P], F32)
        nc.vector.memset(sample_mean[:], 0.0)
        for n in range(SLOTS):
            rows = slice(n * SAMPLE_PARTITIONS, (n + 1) * SAMPLE_PARTITIONS)
            nc.vector.memset(sample_mean[rows, rows], 1.0 / SAMPLE_SIZE)
        table_warmer = const.tile([P, 1], F32)
        nc.scalar.activation(out=table_warmer[:], in_=eps_column[:], func=ACT.Abs_reciprocal_sqrt)

        def transpose_words(words, split):
            banks = []
            for half in range(HALVES):
                bank = ring.tile([P, BANK_PLANES, P], F32, name="word_bank", tag="ring")
                for plane in range(BANK_PLANES):
                    k_pass, u = divmod(half * BANK_PLANES + plane, 2)
                    first = k_pass * 2 * WORDS
                    if split:
                        pair_words = slice(first + u * WORDS, first + (u + 1) * WORDS)
                    else:
                        pair_words = slice(first + u, first + 2 * WORDS, 2)
                    nc.tensor.transpose(bank[:, plane, :], words[:, pair_words], ident_f32[:])
                banks.append(bank)
            return banks

        def regroup(banks):
            grouped = grouped_pool.tile([P, PASSES, P, PACK], BF16, name="grouped", align_bytes=64)
            passes_per_bank = PASSES // HALVES
            for half in range(HALVES):
                first = half * passes_per_bank
                side_by_side = grouped[:].bitcast(F32)[:, first : first + passes_per_bank, :, :]
                planes = banks[half][:].rearrange("p (g u) r -> p g r u", u=PACK // 2)
                nc.scalar.copy(out=side_by_side, in_=planes)
            return grouped

        def quantise(grouped, codes, scales):
            nc.vector.quantize_mx(
                out=codes[:].bitcast(FP8X4),
                scales=scales[:],
                in_=grouped[:].rearrange("p g r t -> p (g r t)"),
            )

        wq_codes = const.tile([P, PASSES * P], U32, align_bytes=64)
        wq_scales = const.tile([P, PASSES * P], U8, align_bytes=64)

        word_banks = {}
        x_split = {}
        grouped_tile = {}
        x_mx = {}
        q_bank = {}
        g_bank = {}
        biased_tile = {}
        y_tile = {}
        kv_t = const.tile([P, SLOTS, CHUNKS, P], BF16)
        row_sums = const.tile([P, CHUNKS], F32)
        mean_columns = const.tile([P, CHUNKS], F32)
        square_sums = const.tile([P, CHUNKS], F32)
        rstd_columns = const.tile([P, CHUNKS], F32)
        sums_bank = sum_psum.tile([P, 2, CHUNKS], F32, name="sums_bank")
        decay_t = const.tile([P, P], BF16)
        bias_all = const.tile([P, P], F32)

        def live(c):
            return 0 <= c < CHUNKS

        def prepare_kv(s):
            kv_bank = qg_psum.tile([P, KV_RUN, P], BF16, name="kv_bank", tag="qg")
            for j in range(KV_RUN):
                nc.tensor.transpose(kv_bank[:, j, :], kv_rows[:, j, s, :], ident_bf16[:])
            nc.vector.tensor_copy(
                out=kv_t[:, s, :, :].rearrange("p c (q j) -> p (c q) j", j=KV_RUN),
                in_=kv_bank[:].rearrange("p j q -> p q j"),
            )

        def prepare_decay():
            decay_bank = qg_psum.tile([P, P], BF16, name="decay_bank", tag="qg")
            nc.tensor.transpose(decay_bank[:], decay_rows[:], ident_bf16[:])
            nc.vector.tensor_copy(out=decay_t[:], in_=decay_bank[:])

        def prepare_bias():
            bias_bank = qg_psum.tile([P, P], F32, name="bias_bank", tag="qg")
            nc.tensor.matmul(out=bias_bank[:], lhsT=ones_bf16[:], rhs=bias_rows[:], start=True, stop=True)
            nc.vector.tensor_copy(out=bias_all[:], in_=bias_bank[:])

        def transposes(c):
            if live(c):
                for s in range(SLOTS):
                    split = (c, s) in x_split
                    rows = x_split[(c, s)] if split else x_rows[(c, s)]
                    word_banks[(c, s)] = transpose_words(rows[:].bitcast(F32), split)

        def split_words(c, s):
            if live(c):
                rows = split_pool.tile([P, E], BF16, name="x_split")
                nc.vector.tensor_copy(
                    out=rows[:].bitcast(F32).rearrange("p (g u w) -> p g u w", g=PASSES, u=2),
                    in_=x_rows[(c, s)][:].bitcast(F32).rearrange("p (g w u) -> p g u w", g=PASSES, u=2),
                )
                x_split[(c, s)] = rows

        def empty_banks(c, s):
            if live(c):
                grouped_tile[(c, s)] = regroup(word_banks[(c, s)])

        def pack(c, s):
            if live(c):
                codes = mx_pool.tile([P, PASSES * P], U32, name="x_codes", align_bytes=64)
                scales = mx_pool.tile([P, PASSES * P], U8, name="x_scales", align_bytes=64)
                quantise(grouped_tile[(c, s)], codes, scales)
                x_mx[(c, s)] = (codes, scales)

        def products(c):
            if not live(c):
                return
            pool, tag = (ring, "ring") if c == CHUNKS - 1 else (qg_psum, "qg")
            qg_bank = pool.tile([P, 2, SLOTS, P], F32, name="qg_bank", tag=tag)
            q_bank[c] = qg_bank[:, 0, :, :]
            g_bank[c] = qg_bank[:, 1, :, :]
            for s in range(SLOTS):
                nc.tensor.matmul(out=g_bank[c][:, s, :], lhsT=kv_t[:, s, c, :], rhs=decay_t[:], start=True, stop=True)
            for s in range(SLOTS):
                codes, scales = x_mx[(c, s)]
                for k_pass in range(PASSES):
                    cols = slice(k_pass * P, (k_pass + 1) * P)
                    nc.tensor.matmul_mx(
                        out=q_bank[c][:, s, :],
                        lhsT=codes[:, cols].bitcast(FP8X4),
                        lhsT_scale=scales[:, cols],
                        rhs=wq_codes[:, cols].bitcast(FP8X4),
                        rhs_scale=wq_scales[:, cols],
                        start=(k_pass == 0),
                        stop=(k_pass == PASSES - 1),
                    )

        def add_bias(c):
            if live(c):
                biased_tile[c] = work.tile([P, SLOTS, P], F32, name="biased")
                nc.vector.tensor_tensor(
                    out=biased_tile[c][:],
                    in0=q_bank[c],
                    in1=bias_all[:].unsqueeze(1).to_broadcast([P, SLOTS, P]),
                    op=ALU.add,
                )

        def weigh(c):
            if live(c):
                y_tile[c] = work.tile([P, SLOTS * P], F32, name="y_tile")
                nc.vector.scalar_tensor_tensor(
                    out=y_tile[c][:],
                    in0=biased_tile[c][:].rearrange("p s q -> p (s q)"),
                    scalar=1.0,
                    in1=g_bank[c].rearrange("p s q -> p (s q)"),
                    op0=ALU.mult,
                    op1=ALU.mult,
                    accum_out=row_sums[:, c : c + 1],
                )

        def mean_of(first, count):
            if live(first):
                chunks = slice(first, first + count)
                nc.tensor.matmul(out=sums_bank[:, 0, chunks], lhsT=sample_mean[:], rhs=row_sums[:, chunks], start=True, stop=True)
                nc.scalar.copy(out=mean_columns[:, chunks], in_=sums_bank[:, 0, chunks])

        def squares(c):
            if live(c):
                squared = work.tile([P, SLOTS * P], F32, name="squared")
                nc.scalar.activation(
                    out=squared[:],
                    in_=y_tile[c][:],
                    func=ACT.Square,
                    bias=mean_columns[:, c : c + 1],
                    scale=-1.0,
                    accum_out=square_sums[:, c : c + 1],
                )

        def deviation_of(first, count, bank):
            if live(first):
                chunks = slice(first, first + count)
                nc.tensor.matmul(out=bank[:, chunks], lhsT=sample_mean[:], rhs=square_sums[:, chunks], start=True, stop=True)
                nc.scalar.activation(
                    out=rstd_columns[:, chunks], in_=bank[:, chunks], func=ACT.Abs_reciprocal_sqrt, bias=eps_column[:]
                )

        def finish(c):
            if live(c):
                res = work.tile([P, SLOTS, P], F32, name="res")
                nc.vector.tensor_scalar(
                    out=res[:].rearrange("p s q -> p (s q)"),
                    in0=y_tile[c][:],
                    scalar1=mean_columns[:, c : c + 1],
                    scalar2=rstd_columns[:, c : c + 1],
                    op0=ALU.subtract,
                    op1=ALU.mult,
                )
                nc.sync.dma_start(out=out_slots[c], in_=res[:])

        with tc.manual_schedule():
            quantise(regroup(transpose_words(wq_rows[:].bitcast(F32), False)), wq_codes, wq_scales)

            for i in range(CHUNKS):
                transposes(i)
                if i == 1:
                    prepare_decay()
                    prepare_bias()
                products(i - 2)
                add_bias(i - 3)
                pack(i - 1, 1)
                if i + 1 in SPLIT:
                    split_words(i + 1, 0)
                empty_banks(i, 0)
                weigh(i - 3)
                pack(i, 0)
                empty_banks(i, 1)
                if i == 0:
                    prepare_kv(0)
                    prepare_kv(1)
                if i == 5 or i == 7:
                    mean_of(i - 5, 2)
                    squares(i - 5)
                    squares(i - 4)
                if i == 6:
                    deviation_of(0, 2, sums_bank[:, 1, :])
            last = CHUNKS - 1
            late_bank = ring.tile([P, CHUNKS], F32, name="late_bank", tag="ring")
            finish(0)
            products(last - 1)
            finish(1)
            mean_of(last - 3, 1)
            pack(last, 1)
            products(last)
            squares(last - 3)
            add_bias(last - 2)
            deviation_of(last - 5, 2, late_bank)
            add_bias(last - 1)
            weigh(last - 2)
            weigh(last - 1)
            mean_of(last - 2, 2)
            squares(last - 2)
            add_bias(last)
            squares(last - 1)
            finish(2)
            weigh(last)
            mean_of(last, 1)
            squares(last)
            deviation_of(last - 3, 3, late_bank)
            deviation_of(last, 1, sums_bank[:, 1, :])
            for c in range(3, CHUNKS):
                finish(c)
